import numpy as np
import ml_dtypes

BF16 = ml_dtypes.bfloat16


def bf(x):
    return np.asarray(x, np.float32).astype(BF16)


def f32(x):
    return np.asarray(x, np.float32)


def f64(x):
    return np.asarray(x).astype(np.float64)


def striped(idx):
    return np.tile(idx.reshape(-1, 16).T, (8, 1))


E, D, H, M, S, N = 64, 128, 256, 512, 4096, 2048


def silu(v):
    return v / (1.0 + np.exp(-v))


def cblock(wr, wi):
    return np.block([[wr, wi], [-wi, wr]])


def setup_inputs():
    table = bf(np.random.standard_normal((D, S)))
    w1 = bf(cblock(np.random.standard_normal((E, H)), np.random.standard_normal((E, H))) / np.sqrt(D))
    b1 = f32(0.1 * np.random.standard_normal((M, 1)))
    w2 = bf(cblock(np.random.standard_normal((H, H)), np.random.standard_normal((H, H))) / np.sqrt(H))
    b2 = f32(0.1 * np.random.standard_normal((M, 1)))
    idx = np.random.permutation(np.tile(np.arange(S), 2))[:N]
    return {"table": table, "w1": w1, "b1": b1, "w2": w2, "b2": b2, "offs": striped(idx)}


def reference(table, w1, b1, w2, b2, offs):
    idx = offs[:16].T.reshape(-1)
    hid = silu(f64(w1).T @ f64(table)[:, idx] + f64(b1))
    return silu(f64(w2).T @ hid + f64(b2))

@@ -1,0 +1,65 @@
+import concourse.mybir as mybir
+
+BF16 = mybir.dt.bfloat16
+F32 = mybir.dt.float32
+U16 = mybir.dt.uint16
+SILU = mybir.ActivationFunctionType.Silu
+
+P = 128
+STEPS = 4096
+WIDTH = 512
+BLOCKS = WIDTH // P
+N = 2048
+PIECE = 512
+PIECES = N // PIECE
+COLS = PIECE // 16
+
+FLOPS = 2 * N * (P * WIDTH + WIDTH * WIDTH)
+
+
+def tile_tfdiff_wifi_lora_kernel(tc, table, w1, b1, w2, b2, offs, out):
+    nc = tc.nc
+    with (
+        tc.tile_pool(name="held", bufs=1) as held,
+        tc.tile_pool(name="stage", bufs=4) as stage,
+        tc.psum_pool(name="psum", bufs=8) as psum,
+    ):
+        offsets = held.tile([P, N // 16], U16, name="offsets")
+        nc.sync.dma_start(offsets[:], offs)
+        w1_sb = held.tile([P, WIDTH], BF16, name="w1_sb")
+        nc.scalar.dma_start(w1_sb[:], w1)
+        table_sb = held.tile([P, STEPS], BF16, name="table_sb")
+        nc.sync.dma_start(table_sb[:], table)
+
+        b1_sb = held.tile([P, BLOCKS], F32, name="b1_sb")
+        b2_sb = held.tile([P, BLOCKS], F32, name="b2_sb")
+        with nc.allow_non_contiguous_dma(reason="512 biases, one to a partition and block"):
+            nc.gpsimd.dma_start(b1_sb[:], b1.rearrange("(c p) o -> p (c o)", p=P))
+            nc.gpsimd.dma_start(b2_sb[:], b2.rearrange("(c p) o -> p (c o)", p=P))
+
+        w2_sb = held.tile([P, BLOCKS, WIDTH], BF16, name="w2_sb")
+        nc.sync.dma_start(w2_sb[:], w2.rearrange("(k p) m -> p k m", p=P))
+
+        hid = [[None] * PIECES for q in range(BLOCKS)]
+        for j in range(PIECES):
+            picked = table_sb[:].indirect(offsets[:, j * COLS : (j + 1) * COLS])
+            for q in range(BLOCKS):
+                acc = psum.tile([P, PIECE], F32, name="acc")
+                nc.tensor.matmul(acc[:], w1_sb[:, q * P : (q + 1) * P], picked, start=True, stop=True)
+                hid[q][j] = held.tile([P, PIECE], BF16, name=f"hid{q}_{j}")
+                nc.scalar.activation(hid[q][j][:], acc[:], SILU, bias=b1_sb[:, q : q + 1])
+
+        for j in range(PIECES):
+            for m in range(BLOCKS):
+                acc = psum.tile([P, PIECE], F32, name="acc")
+                for k in range(BLOCKS):
+                    nc.tensor.matmul(
+                        acc[:],
+                        w2_sb[:, k, m * P : (m + 1) * P],
+                        hid[k][j][:],
+                        start=(k == 0),
+                        stop=(k == BLOCKS - 1),
+                    )
+                res = stage.tile([P, PIECE], F32, name="res")
+                nc.scalar.activation(res[:], acc[:], SILU, bias=b2_sb[:, m : m + 1])
+                nc.sync.dma_start(out[m * P : (m + 1) * P, j * PIECE : (j + 1) * PIECE], res[:])

@@ -24,21 +24,21 @@ def tile_tfdiff_wifi_lora_kernel(tc, table, w1, b1, w2, b2, offs, out):
         tc.tile_pool(name="stage", bufs=4) as stage,
         tc.psum_pool(name="psum", bufs=8) as psum,
     ):
+        table_sb = held.tile([P, STEPS], BF16, name="table_sb")
+        nc.scalar.dma_start(table_sb[:], table)
         offsets = held.tile([P, N // 16], U16, name="offsets")
         nc.sync.dma_start(offsets[:], offs)
         w1_sb = held.tile([P, WIDTH], BF16, name="w1_sb")
-        nc.scalar.dma_start(w1_sb[:], w1)
-        table_sb = held.tile([P, STEPS], BF16, name="table_sb")
-        nc.sync.dma_start(table_sb[:], table)
+        nc.sync.dma_start(w1_sb[:], w1)
 
         b1_sb = held.tile([P, BLOCKS], F32, name="b1_sb")
         b2_sb = held.tile([P, BLOCKS], F32, name="b2_sb")
         with nc.allow_non_contiguous_dma(reason="512 biases, one to a partition and block"):
-            nc.gpsimd.dma_start(b1_sb[:], b1.rearrange("(c p) o -> p (c o)", p=P))
-            nc.gpsimd.dma_start(b2_sb[:], b2.rearrange("(c p) o -> p (c o)", p=P))
+            nc.scalar.dma_start(b1_sb[:], b1.rearrange("(c p) o -> p (c o)", p=P))
+            nc.scalar.dma_start(b2_sb[:], b2.rearrange("(c p) o -> p (c o)", p=P))
 
         w2_sb = held.tile([P, BLOCKS, WIDTH], BF16, name="w2_sb")
-        nc.sync.dma_start(w2_sb[:], w2.rearrange("(k p) m -> p k m", p=P))
+        nc.scalar.dma_start(w2_sb[:], w2.rearrange("(k p) m -> p k m", p=P))
 
         hid = [[None] * PIECES for q in range(BLOCKS)]
         for j in range(PIECES):

@@ -13,6 +13,7 @@ N = 2048
 PIECE = 512
 PIECES = N // PIECE
 COLS = PIECE // 16
+WARM_UP = 10
 
 FLOPS = 2 * N * (P * WIDTH + WIDTH * WIDTH)
 
@@ -39,6 +40,12 @@ def tile_tfdiff_wifi_lora_kernel(tc, table, w1, b1, w2, b2, offs, out):
 
         w2_sb = held.tile([P, BLOCKS, WIDTH], BF16, name="w2_sb")
         nc.scalar.dma_start(w2_sb[:], w2.rearrange("(k p) m -> p k m", p=P))
+
+        zeros = held.tile([P, PIECE], BF16, name="zeros")
+        nc.vector.memset(zeros[:], 0.0)
+        unread = psum.tile([P, PIECE], F32, name="acc")
+        for i in range(WARM_UP):
+            nc.tensor.matmul(unread[:], zeros[:, :P], zeros[:], start=True, stop=True)
 
         hid = [[None] * PIECES for q in range(BLOCKS)]
         for j in range(PIECES):

@@ -13,7 +13,6 @@ N = 2048
 PIECE = 512
 PIECES = N // PIECE
 COLS = PIECE // 16
-WARM_UP = 10
 
 FLOPS = 2 * N * (P * WIDTH + WIDTH * WIDTH)
 
@@ -22,7 +21,7 @@ def tile_tfdiff_wifi_lora_kernel(tc, table, w1, b1, w2, b2, offs, out):
     nc = tc.nc
     with (
         tc.tile_pool(name="held", bufs=1) as held,
-        tc.tile_pool(name="stage", bufs=4) as stage,
+        tc.tile_pool(name="stage", bufs=8) as stage,
         tc.psum_pool(name="psum", bufs=8) as psum,
     ):
         table_sb = held.tile([P, STEPS], BF16, name="table_sb")
@@ -40,12 +39,6 @@ def tile_tfdiff_wifi_lora_kernel(tc, table, w1, b1, w2, b2, offs, out):
 
         w2_sb = held.tile([P, BLOCKS, WIDTH], BF16, name="w2_sb")
         nc.scalar.dma_start(w2_sb[:], w2.rearrange("(k p) m -> p k m", p=P))
-
-        zeros = held.tile([P, PIECE], BF16, name="zeros")
-        nc.vector.memset(zeros[:], 0.0)
-        unread = psum.tile([P, PIECE], F32, name="acc")
-        for i in range(WARM_UP):
-            nc.tensor.matmul(unread[:], zeros[:, :P], zeros[:], start=True, stop=True)
 
         hid = [[None] * PIECES for q in range(BLOCKS)]
         for j in range(PIECES):

@@ -13,6 +13,7 @@ N = 2048
 PIECE = 512
 PIECES = N // PIECE
 COLS = PIECE // 16
+CHUNKS = [(j * PIECE, PIECE) for j in range(PIECES - 1)] + [(N - PIECE, PIECE // 2), (N - PIECE // 2, PIECE // 2)]
 
 FLOPS = 2 * N * (P * WIDTH + WIDTH * WIDTH)
 
@@ -49,17 +50,18 @@ def tile_tfdiff_wifi_lora_kernel(tc, table, w1, b1, w2, b2, offs, out):
                 hid[q][j] = held.tile([P, PIECE], BF16, name=f"hid{q}_{j}")
                 nc.scalar.activation(hid[q][j][:], acc[:], SILU, bias=b1_sb[:, q : q + 1])
 
-        for j in range(PIECES):
+        for start_col, width in CHUNKS:
+            j, inside = divmod(start_col, PIECE)
             for m in range(BLOCKS):
                 acc = psum.tile([P, PIECE], F32, name="acc")
                 for k in range(BLOCKS):
                     nc.tensor.matmul(
-                        acc[:],
+                        acc[:, :width],
                         w2_sb[:, k, m * P : (m + 1) * P],
-                        hid[k][j][:],
+                        hid[k][j][:, inside : inside + width],
                         start=(k == 0),
                         stop=(k == BLOCKS - 1),
                     )
                 res = stage.tile([P, PIECE], F32, name="res")
-                nc.scalar.activation(res[:], acc[:], SILU, bias=b2_sb[:, m : m + 1])
-                nc.sync.dma_start(out[m * P : (m + 1) * P, j * PIECE : (j + 1) * PIECE], res[:])
+                nc.scalar.activation(res[:, :width], acc[:, :width], SILU, bias=b2_sb[:, m : m + 1])
+                nc.sync.dma_start(out[m * P : (m + 1) * P, start_col : start_col + width], res[:, :width])

@@ -4,11 +4,15 @@ BF16 = mybir.dt.bfloat16
 F32 = mybir.dt.float32
 U16 = mybir.dt.uint16
 SILU = mybir.ActivationFunctionType.Silu
+ADD = mybir.AluOpType.add
+SUBTRACT = mybir.AluOpType.subtract
 
 P = 128
 STEPS = 4096
 WIDTH = 512
 BLOCKS = WIDTH // P
+HALF = WIDTH // 2
+HALF_BLOCKS = HALF // P
 N = 2048
 PIECE = 512
 PIECES = N // PIECE
@@ -22,7 +26,7 @@ def tile_tfdiff_wifi_lora_kernel(tc, table, w1, b1, w2, b2, offs, out):
     nc = tc.nc
     with (
         tc.tile_pool(name="held", bufs=1) as held,
-        tc.tile_pool(name="stage", bufs=8) as stage,
+        tc.tile_pool(name="stage", bufs=6) as stage,
         tc.psum_pool(name="psum", bufs=8) as psum,
     ):
         table_sb = held.tile([P, STEPS], BF16, name="table_sb")
@@ -40,8 +44,16 @@ def tile_tfdiff_wifi_lora_kernel(tc, table, w1, b1, w2, b2, offs, out):
 
         w2_sb = held.tile([P, BLOCKS, WIDTH], BF16, name="w2_sb")
         nc.scalar.dma_start(w2_sb[:], w2.rearrange("(k p) m -> p k m", p=P))
+        w_shared = w2_sb[:, 0:HALF_BLOCKS, 0:HALF]
+        w_im = held.tile([P, HALF_BLOCKS, HALF], BF16, name="w_im")
+        nc.vector.tensor_tensor(w_im[:], w2_sb[:, 0:HALF_BLOCKS, HALF:WIDTH], w2_sb[:, 0:HALF_BLOCKS, 0:HALF], SUBTRACT)
+        w_re = held.tile([P, HALF_BLOCKS, HALF], BF16, name="w_re")
+        nc.vector.tensor_tensor(
+            w_re[:], w2_sb[:, HALF_BLOCKS:BLOCKS, 0:HALF], w2_sb[:, HALF_BLOCKS:BLOCKS, HALF:WIDTH], SUBTRACT
+        )
 
         hid = [[None] * PIECES for q in range(BLOCKS)]
+        hid_sum = [[None] * PIECES for k in range(HALF_BLOCKS)]
         for j in range(PIECES):
             picked = table_sb[:].indirect(offsets[:, j * COLS : (j + 1) * COLS])
             for q in range(BLOCKS):
@@ -49,19 +61,48 @@ def tile_tfdiff_wifi_lora_kernel(tc, table, w1, b1, w2, b2, offs, out):
                 nc.tensor.matmul(acc[:], w1_sb[:, q * P : (q + 1) * P], picked, start=True, stop=True)
                 hid[q][j] = held.tile([P, PIECE], BF16, name=f"hid{q}_{j}")
                 nc.scalar.activation(hid[q][j][:], acc[:], SILU, bias=b1_sb[:, q : q + 1])
+            for k in range(HALF_BLOCKS):
+                hid_sum[k][j] = held.tile([P, PIECE], BF16, name=f"hid_sum{k}_{j}")
+                nc.vector.tensor_tensor(hid_sum[k][j][:], hid[k][j][:], hid[HALF_BLOCKS + k][j][:], ADD)
+        hid_re = hid[0:HALF_BLOCKS]
+        hid_im = hid[HALF_BLOCKS:BLOCKS]
 
-        for start_col, width in CHUNKS:
+        def product(weights, moving, m, start_col, width):
             j, inside = divmod(start_col, PIECE)
-            for m in range(BLOCKS):
-                acc = psum.tile([P, PIECE], F32, name="acc")
-                for k in range(BLOCKS):
-                    nc.tensor.matmul(
-                        acc[:, :width],
-                        w2_sb[:, k, m * P : (m + 1) * P],
-                        hid[k][j][:, inside : inside + width],
-                        start=(k == 0),
-                        stop=(k == BLOCKS - 1),
-                    )
+            acc = psum.tile([P, PIECE], F32, name="acc")
+            for k in range(HALF_BLOCKS):
+                nc.tensor.matmul(
+                    acc[:, :width],
+                    weights[:, k, m * P : (m + 1) * P],
+                    moving[k][j][:, inside : inside + width],
+                    start=(k == 0),
+                    stop=(k == HALF_BLOCKS - 1),
+                )
+            return acc
+
+        units = [(start_col, width, m) for start_col, width in CHUNKS for m in range(HALF_BLOCKS)]
+
+        def shared_product(start_col, width, m):
+            shared = product(w_shared, hid_sum, m, start_col, width)
+            shared_sb = stage.tile([P, PIECE], F32, name="shared_sb")
+            if m % 2 == 0:
+                nc.vector.tensor_copy(shared_sb[:, :width], shared[:, :width])
+            else:
+                nc.scalar.copy(shared_sb[:, :width], shared[:, :width])
+            return shared_sb
+
+        def both_parts(shared_sb, start_col, width, m):
+            for weights, moving, block in ((w_im[:], hid_re, HALF_BLOCKS + m), (w_re[:], hid_im, m)):
+                own = product(weights, moving, m, start_col, width)
+                pre = stage.tile([P, PIECE], F32, name="pre")
+                nc.vector.tensor_tensor(pre[:, :width], own[:, :width], shared_sb[:, :width], ADD)
                 res = stage.tile([P, PIECE], F32, name="res")
-                nc.scalar.activation(res[:, :width], acc[:, :width], SILU, bias=b2_sb[:, m : m + 1])
-                nc.sync.dma_start(out[m * P : (m + 1) * P, start_col : start_col + width], res[:, :width])
+                nc.scalar.activation(res[:, :width], pre[:, :width], SILU, bias=b2_sb[:, block : block + 1])
+                nc.sync.dma_start(out[block * P : (block + 1) * P, start_col : start_col + width], res[:, :width])
+
+        ahead = shared_product(*units[0])
+        for u, unit in enumerate(units):
+            shared_sb = ahead
+            if u + 1 < len(units):
+                ahead = shared_product(*units[u + 1])
+            both_parts(shared_sb, *unit)

@@ -39,11 +39,11 @@ def tile_tfdiff_wifi_lora_kernel(tc, table, w1, b1, w2, b2, offs, out):
         b1_sb = held.tile([P, BLOCKS], F32, name="b1_sb")
         b2_sb = held.tile([P, BLOCKS], F32, name="b2_sb")
         with nc.allow_non_contiguous_dma(reason="512 biases, one to a partition and block"):
-            nc.scalar.dma_start(b1_sb[:], b1.rearrange("(c p) o -> p (c o)", p=P))
-            nc.scalar.dma_start(b2_sb[:], b2.rearrange("(c p) o -> p (c o)", p=P))
+            nc.sync.dma_start(b1_sb[:], b1.rearrange("(c p) o -> p (c o)", p=P))
+            nc.sync.dma_start(b2_sb[:], b2.rearrange("(c p) o -> p (c o)", p=P))
 
         w2_sb = held.tile([P, BLOCKS, WIDTH], BF16, name="w2_sb")
-        nc.scalar.dma_start(w2_sb[:], w2.rearrange("(k p) m -> p k m", p=P))
+        nc.sync.dma_start(w2_sb[:], w2.rearrange("(k p) m -> p k m", p=P))
         w_shared = w2_sb[:, 0:HALF_BLOCKS, 0:HALF]
         w_im = held.tile([P, HALF_BLOCKS, HALF], BF16, name="w_im")
         nc.vector.tensor_tensor(w_im[:], w2_sb[:, 0:HALF_BLOCKS, HALF:WIDTH], w2_sb[:, 0:HALF_BLOCKS, 0:HALF], SUBTRACT)

@@ -26,7 +26,7 @@ def tile_tfdiff_wifi_lora_kernel(tc, table, w1, b1, w2, b2, offs, out):
     nc = tc.nc
     with (
         tc.tile_pool(name="held", bufs=1) as held,
-        tc.tile_pool(name="stage", bufs=6) as stage,
+        tc.tile_pool(name="stage", bufs=12) as stage,
         tc.psum_pool(name="psum", bufs=8) as psum,
     ):
         table_sb = held.tile([P, STEPS], BF16, name="table_sb")

@@ -43,7 +43,7 @@ def tile_tfdiff_wifi_lora_kernel(tc, table, w1, b1, w2, b2, offs, out):
             nc.sync.dma_start(b2_sb[:], b2.rearrange("(c p) o -> p (c o)", p=P))
 
         w2_sb = held.tile([P, BLOCKS, WIDTH], BF16, name="w2_sb")
-        nc.sync.dma_start(w2_sb[:], w2.rearrange("(k p) m -> p k m", p=P))
+        nc.scalar.dma_start(w2_sb[:], w2.rearrange("(k p) m -> p k m", p=P))
         w_shared = w2_sb[:, 0:HALF_BLOCKS, 0:HALF]
         w_im = held.tile([P, HALF_BLOCKS, HALF], BF16, name="w_im")
         nc.vector.tensor_tensor(w_im[:], w2_sb[:, 0:HALF_BLOCKS, HALF:WIDTH], w2_sb[:, 0:HALF_BLOCKS, 0:HALF], SUBTRACT)

@@ -63,7 +63,7 @@ def tile_tfdiff_wifi_lora_kernel(tc, table, w1, b1, w2, b2, offs, out):
                 nc.scalar.activation(hid[q][j][:], acc[:], SILU, bias=b1_sb[:, q : q + 1])
             for k in range(HALF_BLOCKS):
                 hid_sum[k][j] = held.tile([P, PIECE], BF16, name=f"hid_sum{k}_{j}")
-                nc.vector.tensor_tensor(hid_sum[k][j][:], hid[k][j][:], hid[HALF_BLOCKS + k][j][:], ADD)
+                nc.gpsimd.tensor_tensor(hid_sum[k][j][:], hid[k][j][:], hid[HALF_BLOCKS + k][j][:], ADD)
         hid_re = hid[0:HALF_BLOCKS]
         hid_im = hid[HALF_BLOCKS:BLOCKS]
 
@@ -85,10 +85,7 @@ def tile_tfdiff_wifi_lora_kernel(tc, table, w1, b1, w2, b2, offs, out):
         def shared_product(start_col, width, m):
             shared = product(w_shared, hid_sum, m, start_col, width)
             shared_sb = stage.tile([P, PIECE], F32, name="shared_sb")
-            if m % 2 == 0:
-                nc.vector.tensor_copy(shared_sb[:, :width], shared[:, :width])
-            else:
-                nc.scalar.copy(shared_sb[:, :width], shared[:, :width])
+            nc.vector.tensor_copy(shared_sb[:, :width], shared[:, :width])
             return shared_sb
 
         def both_parts(shared_sb, start_col, width, m):

@@ -17,7 +17,7 @@ N = 2048
 PIECE = 512
 PIECES = N // PIECE
 COLS = PIECE // 16
-CHUNKS = [(j * PIECE, PIECE) for j in range(PIECES - 1)] + [(N - PIECE, PIECE // 2), (N - PIECE // 2, PIECE // 2)]
+CHUNKS = [(j * PIECE, PIECE) for j in range(PIECES)]
 
 FLOPS = 2 * N * (P * WIDTH + WIDTH * WIDTH)
 

@@ -17,6 +17,7 @@ N = 2048
 PIECE = 512
 PIECES = N // PIECE
 COLS = PIECE // 16
+BANKS = 8
 CHUNKS = [(j * PIECE, PIECE) for j in range(PIECES)]
 
 FLOPS = 2 * N * (P * WIDTH + WIDTH * WIDTH)
@@ -26,9 +27,16 @@ def tile_tfdiff_wifi_lora_kernel(tc, table, w1, b1, w2, b2, offs, out):
     nc = tc.nc
     with (
         tc.tile_pool(name="held", bufs=1) as held,
-        tc.tile_pool(name="stage", bufs=12) as stage,
-        tc.psum_pool(name="psum", bufs=8) as psum,
+        tc.psum_pool(name="psum", bufs=1) as psum,
     ):
+        banks = [psum.tile([P, PIECE], F32, name=f"bank{b}") for b in range(BANKS)]
+        taken = []
+
+        def next_bank():
+            bank = banks[len(taken) % BANKS]
+            taken.append(bank)
+            return bank
+
         table_sb = held.tile([P, STEPS], BF16, name="table_sb")
         nc.scalar.dma_start(table_sb[:], table)
         offsets = held.tile([P, N // 16], U16, name="offsets")
@@ -57,7 +65,7 @@ def tile_tfdiff_wifi_lora_kernel(tc, table, w1, b1, w2, b2, offs, out):
         for j in range(PIECES):
             picked = table_sb[:].indirect(offsets[:, j * COLS : (j + 1) * COLS])
             for q in range(BLOCKS):
-                acc = psum.tile([P, PIECE], F32, name="acc")
+                acc = next_bank()
                 nc.tensor.matmul(acc[:], w1_sb[:, q * P : (q + 1) * P], picked, start=True, stop=True)
                 hid[q][j] = held.tile([P, PIECE], BF16, name=f"hid{q}_{j}")
                 nc.scalar.activation(hid[q][j][:], acc[:], SILU, bias=b1_sb[:, q : q + 1])
@@ -69,7 +77,7 @@ def tile_tfdiff_wifi_lora_kernel(tc, table, w1, b1, w2, b2, offs, out):
 
         def product(weights, moving, m, start_col, width):
             j, inside = divmod(start_col, PIECE)
-            acc = psum.tile([P, PIECE], F32, name="acc")
+            acc = next_bank()
             for k in range(HALF_BLOCKS):
                 nc.tensor.matmul(
                     acc[:, :width],
@@ -84,16 +92,16 @@ def tile_tfdiff_wifi_lora_kernel(tc, table, w1, b1, w2, b2, offs, out):
 
         def shared_product(start_col, width, m):
             shared = product(w_shared, hid_sum, m, start_col, width)
-            shared_sb = stage.tile([P, PIECE], F32, name="shared_sb")
+            shared_sb = held.tile([P, PIECE], F32, name=f"shared_sb{m}_{start_col}")
             nc.vector.tensor_copy(shared_sb[:, :width], shared[:, :width])
             return shared_sb
 
         def both_parts(shared_sb, start_col, width, m):
             for weights, moving, block in ((w_im[:], hid_re, HALF_BLOCKS + m), (w_re[:], hid_im, m)):
                 own = product(weights, moving, m, start_col, width)
-                pre = stage.tile([P, PIECE], F32, name="pre")
+                pre = held.tile([P, PIECE], F32, name=f"pre{block}_{start_col}")
                 nc.vector.tensor_tensor(pre[:, :width], own[:, :width], shared_sb[:, :width], ADD)
-                res = stage.tile([P, PIECE], F32, name="res")
+                res = held.tile([P, PIECE], F32, name=f"res{block}_{start_col}")
                 nc.scalar.activation(res[:, :width], pre[:, :width], SILU, bias=b2_sb[:, block : block + 1])
                 nc.sync.dma_start(out[block * P : (block + 1) * P, start_col : start_col + width], res[:, :width])
 

@@ -105,9 +105,27 @@ def tile_tfdiff_wifi_lora_kernel(tc, table, w1, b1, w2, b2, offs, out):
                 nc.scalar.activation(res[:, :width], pre[:, :width], SILU, bias=b2_sb[:, block : block + 1])
                 nc.sync.dma_start(out[block * P : (block + 1) * P, start_col : start_col + width], res[:, :width])
 
-        ahead = shared_product(*units[0])
-        for u, unit in enumerate(units):
+        def both_parts_direct(start_col, width, m):
+            j, inside = divmod(start_col, PIECE)
+            for block in (HALF_BLOCKS + m, m):
+                acc = next_bank()
+                for k in range(BLOCKS):
+                    nc.tensor.matmul(
+                        acc[:, :width],
+                        w2_sb[:, k, block * P : (block + 1) * P],
+                        hid[k][j][:, inside : inside + width],
+                        start=(k == 0),
+                        stop=(k == BLOCKS - 1),
+                    )
+                res = held.tile([P, PIECE], F32, name=f"res{block}_{start_col}")
+                nc.scalar.activation(res[:, :width], acc[:, :width], SILU, bias=b2_sb[:, block : block + 1])
+                nc.sync.dma_start(out[block * P : (block + 1) * P, start_col : start_col + width], res[:, :width])
+
+        three_product_units = units[:-1]
+        ahead = shared_product(*three_product_units[0])
+        for u, unit in enumerate(three_product_units):
             shared_sb = ahead
-            if u + 1 < len(units):
-                ahead = shared_product(*units[u + 1])
+            if u + 1 < len(three_product_units):
+                ahead = shared_product(*three_product_units[u + 1])
             both_parts(shared_sb, *unit)
+        both_parts_direct(*units[-1])

@@ -41,8 +41,11 @@ def tile_tfdiff_wifi_lora_kernel(tc, table, w1, b1, w2, b2, offs, out):
         nc.scalar.dma_start(table_sb[:], table)
         offsets = held.tile([P, N // 16], U16, name="offsets")
         nc.sync.dma_start(offsets[:], offs)
-        w1_sb = held.tile([P, WIDTH], BF16, name="w1_sb")
-        nc.sync.dma_start(w1_sb[:], w1)
+        w1_first = held.tile([P, P], BF16, name="w1_first")
+        nc.sync.dma_start(w1_first[:], w1[:, 0:P])
+        w1_rest = held.tile([P, WIDTH - P], BF16, name="w1_rest")
+        nc.scalar.dma_start(w1_rest[:], w1[:, P:WIDTH])
+        w1_blocks = [w1_first[:]] + [w1_rest[:, (q - 1) * P : q * P] for q in range(1, BLOCKS)]
 
         b1_sb = held.tile([P, BLOCKS], F32, name="b1_sb")
         b2_sb = held.tile([P, BLOCKS], F32, name="b2_sb")
@@ -66,7 +69,7 @@ def tile_tfdiff_wifi_lora_kernel(tc, table, w1, b1, w2, b2, offs, out):
             picked = table_sb[:].indirect(offsets[:, j * COLS : (j + 1) * COLS])
             for q in range(BLOCKS):
                 acc = next_bank()
-                nc.tensor.matmul(acc[:], w1_sb[:, q * P : (q + 1) * P], picked, start=True, stop=True)
+                nc.tensor.matmul(acc[:], w1_blocks[q], picked, start=True, stop=True)
                 hid[q][j] = held.tile([P, PIECE], BF16, name=f"hid{q}_{j}")
                 nc.scalar.activation(hid[q][j][:], acc[:], SILU, bias=b1_sb[:, q : q + 1])
             for k in range(HALF_BLOCKS):

import concourse.mybir as mybir

BF16 = mybir.dt.bfloat16
F32 = mybir.dt.float32
U16 = mybir.dt.uint16
SILU = mybir.ActivationFunctionType.Silu
ADD = mybir.AluOpType.add
SUBTRACT = mybir.AluOpType.subtract

P = 128
STEPS = 4096
WIDTH = 512
BLOCKS = WIDTH // P
HALF = WIDTH // 2
HALF_BLOCKS = HALF // P
N = 2048
PIECE = 512
PIECES = N // PIECE
COLS = PIECE // 16
BANKS = 8
CHUNKS = [(j * PIECE, PIECE) for j in range(PIECES)]

FLOPS = 2 * N * (P * WIDTH + WIDTH * WIDTH)


def tile_tfdiff_wifi_lora_kernel(tc, table, w1, b1, w2, b2, offs, out):
    nc = tc.nc
    with (
        tc.tile_pool(name="held", bufs=1) as held,
        tc.psum_pool(name="psum", bufs=1) as psum,
    ):
        banks = [psum.tile([P, PIECE], F32, name=f"bank{b}") for b in range(BANKS)]
        taken = []

        def next_bank():
            bank = banks[len(taken) % BANKS]
            taken.append(bank)
            return bank

        table_sb = held.tile([P, STEPS], BF16, name="table_sb")
        nc.scalar.dma_start(table_sb[:], table)
        offsets = held.tile([P, N // 16], U16, name="offsets")
        nc.sync.dma_start(offsets[:], offs)
        w1_first = held.tile([P, P], BF16, name="w1_first")
        nc.sync.dma_start(w1_first[:], w1[:, 0:P])
        w1_rest = held.tile([P, WIDTH - P], BF16, name="w1_rest")
        nc.scalar.dma_start(w1_rest[:], w1[:, P:WIDTH])
        w1_blocks = [w1_first[:]] + [w1_rest[:, (q - 1) * P : q * P] for q in range(1, BLOCKS)]

        b1_sb = held.tile([P, BLOCKS], F32, name="b1_sb")
        b2_sb = held.tile([P, BLOCKS], F32, name="b2_sb")
        with nc.allow_non_contiguous_dma(reason="512 biases, one to a partition and block"):
            nc.sync.dma_start(b1_sb[:], b1.rearrange("(c p) o -> p (c o)", p=P))
            nc.sync.dma_start(b2_sb[:], b2.rearrange("(c p) o -> p (c o)", p=P))

        w2_sb = held.tile([P, BLOCKS, WIDTH], BF16, name="w2_sb")
        nc.scalar.dma_start(w2_sb[:], w2.rearrange("(k p) m -> p k m", p=P))
        w_shared = w2_sb[:, 0:HALF_BLOCKS, 0:HALF]
        w_im = held.tile([P, HALF_BLOCKS, HALF], BF16, name="w_im")
        nc.vector.tensor_tensor(w_im[:], w2_sb[:, 0:HALF_BLOCKS, HALF:WIDTH], w2_sb[:, 0:HALF_BLOCKS, 0:HALF], SUBTRACT)
        w_re = held.tile([P, HALF_BLOCKS, HALF], BF16, name="w_re")
        nc.vector.tensor_tensor(
            w_re[:], w2_sb[:, HALF_BLOCKS:BLOCKS, 0:HALF], w2_sb[:, HALF_BLOCKS:BLOCKS, HALF:WIDTH], SUBTRACT
        )

        hid = [[None] * PIECES for q in range(BLOCKS)]
        hid_sum = [[None] * PIECES for k in range(HALF_BLOCKS)]
        for j in range(PIECES):
            picked = table_sb[:].indirect(offsets[:, j * COLS : (j + 1) * COLS])
            for q in range(BLOCKS):
                acc = next_bank()
                nc.tensor.matmul(acc[:], w1_blocks[q], picked, start=True, stop=True)
                hid[q][j] = held.tile([P, PIECE], BF16, name=f"hid{q}_{j}")
                nc.scalar.activation(hid[q][j][:], acc[:], SILU, bias=b1_sb[:, q : q + 1])
            for k in range(HALF_BLOCKS):
                hid_sum[k][j] = held.tile([P, PIECE], BF16, name=f"hid_sum{k}_{j}")
                nc.gpsimd.tensor_tensor(hid_sum[k][j][:], hid[k][j][:], hid[HALF_BLOCKS + k][j][:], ADD)
        hid_re = hid[0:HALF_BLOCKS]
        hid_im = hid[HALF_BLOCKS:BLOCKS]

        def product(weights, moving, m, start_col, width):
            j, inside = divmod(start_col, PIECE)
            acc = next_bank()
            for k in range(HALF_BLOCKS):
                nc.tensor.matmul(
                    acc[:, :width],
                    weights[:, k, m * P : (m + 1) * P],
                    moving[k][j][:, inside : inside + width],
                    start=(k == 0),
                    stop=(k == HALF_BLOCKS - 1),
                )
            return acc

        units = [(start_col, width, m) for start_col, width in CHUNKS for m in range(HALF_BLOCKS)]

        def shared_product(start_col, width, m):
            shared = product(w_shared, hid_sum, m, start_col, width)
            shared_sb = held.tile([P, PIECE], F32, name=f"shared_sb{m}_{start_col}")
            nc.vector.tensor_copy(shared_sb[:, :width], shared[:, :width])
            return shared_sb

        def both_parts(shared_sb, start_col, width, m):
            for weights, moving, block in ((w_im[:], hid_re, HALF_BLOCKS + m), (w_re[:], hid_im, m)):
                own = product(weights, moving, m, start_col, width)
                pre = held.tile([P, PIECE], F32, name=f"pre{block}_{start_col}")
                nc.vector.tensor_tensor(pre[:, :width], own[:, :width], shared_sb[:, :width], ADD)
                res = held.tile([P, PIECE], F32, name=f"res{block}_{start_col}")
                nc.scalar.activation(res[:, :width], pre[:, :width], SILU, bias=b2_sb[:, block : block + 1])
                nc.sync.dma_start(out[block * P : (block + 1) * P, start_col : start_col + width], res[:, :width])

        def both_parts_direct(start_col, width, m):
            j, inside = divmod(start_col, PIECE)
            for block in (HALF_BLOCKS + m, m):
                acc = next_bank()
                for k in range(BLOCKS):
                    nc.tensor.matmul(
                        acc[:, :width],
                        w2_sb[:, k, block * P : (block + 1) * P],
                        hid[k][j][:, inside : inside + width],
                        start=(k == 0),
                        stop=(k == BLOCKS - 1),
                    )
                res = held.tile([P, PIECE], F32, name=f"res{block}_{start_col}")
                nc.scalar.activation(res[:, :width], acc[:, :width], SILU, bias=b2_sb[:, block : block + 1])
                nc.sync.dma_start(out[block * P : (block + 1) * P, start_col : start_col + width], res[:, :width])

        three_product_units = units[:-1]
        ahead = shared_product(*three_product_units[0])
        for u, unit in enumerate(three_product_units):
            shared_sb = ahead
            if u + 1 < len(three_product_units):
                ahead = shared_product(*three_product_units[u + 1])
            both_parts(shared_sb, *unit)
        both_parts_direct(*units[-1])
